import numpy as np
import ml_dtypes


def mxq(x, axis, fmt="e4m3"):
    dtype, down = {"e4m3": (ml_dtypes.float8_e4m3fn, 7), "e5m2": (ml_dtypes.float8_e5m2, 14)}[fmt]
    v = np.moveaxis(np.asarray(x, np.float32).astype(ml_dtypes.bfloat16).astype(np.float64), axis, -1)
    blocks = v.reshape(v.shape[:-1] + (-1, 32))
    amax = np.abs(blocks).max(-1, keepdims=True)
    byte = np.maximum(np.where(amax > 0, np.frexp(amax)[1] - 1 + 127, 0) - down, 1)
    scale = np.exp2(byte - 127.0)
    codes = (blocks / scale).astype(np.float32).astype(dtype).astype(np.float64)
    return np.moveaxis((codes * scale).reshape(v.shape), -1, axis)


WIDE = False


def mx_kscale(k):
    if not WIDE:
        return np.ones(k)
    levels = np.array([10, -10, 5, -5, 0])
    a = np.random.permutation(np.resize(levels, k // 512 * 4)).reshape(k // 512, 4)
    idx = np.arange(k)
    return np.exp2(a[idx // 512, idx % 128 // 32])


BF16 = ml_dtypes.bfloat16


def bf(x):
    return np.asarray(x, np.float32).astype(BF16)


def f64(x):
    return np.asarray(x).astype(np.float64)


B, L, C, D, H, Q = 8, 1024, 512, 256, 8, 256
EPS = 1e-5


def layer_norm(v, w, b):
    mu = v.mean(-1, keepdims=True)
    var = v.var(-1, keepdims=True)
    return (v - mu) * (1.0 / np.sqrt(var + EPS)) * w + b


def setup_inputs():
    s = mx_kscale(C)
    mag = 10.0 ** (-2.5 * np.random.uniform(size=(B, L, 1)))
    x = (np.random.standard_normal((B, L, C)) + 0.5 * np.random.standard_normal((B, L, 1))) * mag
    return {"x": bf(x),
            "ln_k_w": bf((1.0 + 0.1 * np.random.standard_normal(C)) * s),
            "ln_k_b": bf(0.1 * np.random.standard_normal(C) * s),
            "Wk": bf(np.random.standard_normal((D, C)) / np.sqrt(C) / s[None, :]),
            "Wv": bf(np.random.standard_normal((D, C)) / np.sqrt(C) / s[None, :]),
            "bk": bf(0.1 * np.random.standard_normal(D)),
            "bv": bf(0.1 * np.random.standard_normal(D))}


def reference(x, ln_k_w, ln_k_b, Wk, Wv, bk, bv):
    xk = mxq(layer_norm(f64(x), f64(ln_k_w), f64(ln_k_b)), 2, "e4m3")
    k = (xk @ mxq(f64(Wk).T, 0, "e4m3")) + f64(bk)
    v = (xk @ mxq(f64(Wv).T, 0, "e4m3")) + f64(bv)
    return k, v

@@ -1,0 +1,174 @@
+from contextlib import ExitStack
+
+import concourse.mybir as mybir
+from concourse.masks import make_identity
+
+FP32 = mybir.dt.float32
+BF16 = mybir.dt.bfloat16
+U32 = mybir.dt.uint32
+U8 = mybir.dt.uint8
+FP8X4 = mybir.dt.float8_e4m3fn_x4
+ALU = mybir.AluOpType
+ACT = mybir.ActivationFunctionType
+
+P = 128
+PACK = 4
+FEATS = 512
+TOKENS = 8192
+HALF = 256
+OUTS = 2 * HALF
+NT = 4
+GROUP = NT * P
+NG = TOKENS // GROUP
+EPS = 1e-5
+
+FLOPS = 2 * TOKENS * FEATS * OUTS
+
+
+def tile_attentionalpoolerwmasking_pa_t_kernel(tc, x, ln_k_w, ln_k_b, Wk, Wv, bk, bv, out_0, out_1):
+    nc = tc.nc
+    xf = x.flatten_outer_dims()
+    kf = out_0.flatten_outer_dims()
+    vf = out_1.flatten_outer_dims()
+
+    with ExitStack() as ctx:
+        const = ctx.enter_context(tc.tile_pool(name="const", bufs=1))
+        xin = ctx.enter_context(tc.tile_pool(name="xin", bufs=NG))
+        small = ctx.enter_context(tc.tile_pool(name="small", bufs=6))
+        xh = ctx.enter_context(tc.tile_pool(name="xh", bufs=3))
+        pl = ctx.enter_context(tc.tile_pool(name="pl", bufs=3))
+        gr = ctx.enter_context(tc.tile_pool(name="gr", bufs=3))
+        cd = ctx.enter_context(tc.tile_pool(name="cd", bufs=3))
+        rs = ctx.enter_context(tc.tile_pool(name="rs", bufs=4))
+        psum = ctx.enter_context(tc.psum_pool(name="psum", bufs=4))
+
+        x_tiles = []
+        for g in range(NG):
+            x_sb = xin.tile([P, NT, FEATS], BF16, tag="x", name="x_sb%d" % g)
+            x_tiles.append(x_sb)
+        nc.sync.dma_start(out=x_tiles[0][:], in_=xf[0:GROUP, :].rearrange("(p n) f -> p n f", n=NT))
+
+        w_raw = const.tile([P, 4, FEATS], BF16)
+        nc.scalar.dma_start(out=w_raw[:, 0:2, :], in_=Wk.rearrange("(c p) f -> p c f", p=P))
+        nc.scalar.dma_start(out=w_raw[:, 2:4, :], in_=Wv.rearrange("(c p) f -> p c f", p=P))
+        ln_rows = const.tile([P, P], BF16)
+        nc.vector.memset(ln_rows[:], 0.0)
+        nc.scalar.dma_start(out=ln_rows[0:4, :], in_=ln_k_w.rearrange("(j p) -> j p", p=P))
+        nc.scalar.dma_start(out=ln_rows[4:8, :], in_=ln_k_b.rearrange("(j p) -> j p", p=P))
+        bias_sb = const.tile([P, OUTS], BF16)
+        nc.scalar.dma_start(out=bias_sb[:, 0:HALF], in_=bk.partition_broadcast(P))
+        nc.scalar.dma_start(out=bias_sb[:, HALF:OUTS], in_=bv.partition_broadcast(P))
+
+        for g in range(1, NG):
+            nc.sync.dma_start(
+                out=x_tiles[g][:], in_=xf[g * GROUP : (g + 1) * GROUP, :].rearrange("(p n) f -> p n f", n=NT)
+            )
+
+        ident_f = const.tile([P, P], FP32)
+        make_identity(nc, ident_f[:])
+        ident_b = const.tile([P, P], BF16)
+        make_identity(nc, ident_b[:])
+
+        w_grp = const.tile([P, OUTS, PACK], BF16, align_bytes=64)
+        for h in range(2):
+            wt = psum.tile([P, PACK, HALF], BF16, tag="t", name="wt%d" % h)
+            for j in range(PACK):
+                for c in range(2):
+                    nc.tensor.transpose(
+                        wt[:, j, c * P : (c + 1) * P], w_raw[:, 2 * h + c, j * P : (j + 1) * P], ident_b[:]
+                    )
+            nc.vector.tensor_copy(
+                out=w_grp[:, h * HALF : (h + 1) * HALF, :], in_=wt[:].rearrange("p j o -> p o j")
+            )
+        w_codes = const.tile([P, OUTS], U32, align_bytes=64)
+        w_scales = const.tile([P, OUTS], U8, align_bytes=64)
+        nc.vector.quantize_mx(
+            out=w_codes[:].bitcast(FP8X4), scales=w_scales[:], in_=w_grp[:].rearrange("p o j -> p (o j)")
+        )
+
+        ln_t = psum.tile([P, P], BF16, tag="t")
+        nc.tensor.transpose(ln_t[:], ln_rows[:], ident_b[:])
+        ln_col = const.tile([P, 8], FP32)
+        nc.vector.tensor_copy(out=ln_col[:], in_=ln_t[:, 0:8])
+
+        for g in range(NG):
+            x_sb = x_tiles[g]
+            stats = small.tile([P, NT, 6], FP32)
+            mv = small.tile([P, NT, 2], FP32)
+            for n in range(NT):
+                nc.vector.bn_stats(out=stats[:, n, :], in_=x_sb[:, n, :])
+            for n in range(NT):
+                nc.vector.bn_aggr(out=mv[:, n, :], in_=stats[:, n, :])
+            std = small.tile([P, NT], FP32)
+            nc.scalar.activation(out=std[:], in_=mv[:, :, 1], func=ACT.Sqrt, bias=EPS, scale=1.0)
+            rstd = small.tile([P, NT], FP32)
+            nc.vector.reciprocal(out=rstd[:], in_=std[:])
+            negm = small.tile([P, NT], FP32)
+            nc.gpsimd.tensor_scalar(
+                out=negm[:], in0=mv[:, :, 0], scalar1=-1.0, scalar2=0.0, op0=ALU.mult, op1=ALU.add
+            )
+
+            xhat = xh.tile([P, NT, FEATS], FP32)
+            for n in range(NT):
+                nc.gpsimd.tensor_scalar(
+                    out=xhat[:, n, :],
+                    in0=x_sb[:, n, :],
+                    scalar1=negm[:, n : n + 1],
+                    scalar2=rstd[:, n : n + 1],
+                    op0=ALU.add,
+                    op1=ALU.mult,
+                )
+
+            banks = []
+            for j in range(PACK):
+                tb = psum.tile([P, GROUP], FP32, tag="t", name="tb%d" % j)
+                banks.append(tb)
+            for n in range(NT):
+                for j in range(PACK):
+                    nc.tensor.transpose(
+                        banks[j][:, n * P : (n + 1) * P], xhat[:, n, j * P : (j + 1) * P], ident_f[:]
+                    )
+
+            planes = pl.tile([P, PACK, GROUP], BF16)
+            for j in range(PACK):
+                nc.scalar.activation(
+                    out=planes[:, j, :],
+                    in_=banks[j][:],
+                    func=ACT.Identity,
+                    scale=ln_col[:, j : j + 1],
+                    bias=ln_col[:, PACK + j : PACK + j + 1],
+                )
+
+            grouped = gr.tile([P, GROUP, PACK], BF16, align_bytes=64)
+            nc.scalar.copy(
+                out=grouped[:].rearrange("p (c i) t -> p c t i", i=4),
+                in_=planes[:].rearrange("p t (c i) -> p c t i", i=4),
+            )
+
+            codes = cd.tile([P, GROUP], U32, align_bytes=64)
+            scl = cd.tile([P, GROUP], U8, align_bytes=64)
+            nc.vector.quantize_mx(
+                out=codes[:].bitcast(FP8X4), scales=scl[:], in_=grouped[:].rearrange("p c t -> p (c t)")
+            )
+
+            res = rs.tile([P, 2, NT, HALF], FP32)
+            for n in range(NT):
+                ob = psum.tile([P, OUTS], FP32, tag="o")
+                nc.tensor.matmul_mx(
+                    out=ob[:],
+                    lhsT=codes[:, n * P : (n + 1) * P].bitcast(FP8X4),
+                    lhsT_scale=scl[:, n * P : (n + 1) * P],
+                    rhs=w_codes[:].bitcast(FP8X4),
+                    rhs_scale=w_scales[:],
+                    start=True,
+                    stop=True,
+                )
+                nc.vector.tensor_tensor(
+                    out=res[:, :, n, :],
+                    in0=ob[:].rearrange("p (h o) -> p h o", h=2),
+                    in1=bias_sb[:].rearrange("p (h o) -> p h o", h=2),
+                    op=ALU.add,
+                )
+            rows = slice(g * GROUP, (g + 1) * GROUP)
+            nc.sync.dma_start(out=kf[rows, :].rearrange("(p n) o -> p n o", n=NT), in_=res[:, 0, :, :])
+            nc.sync.dma_start(out=vf[rows, :].rearrange("(p n) o -> p n o", n=NT), in_=res[:, 1, :, :])

@@ -21,8 +21,19 @@ NT = 4
 GROUP = NT * P
 NG = TOKENS // GROUP
 EPS = 1e-5
+LC = 2
+LE = 3
+LQ = 4
 
 FLOPS = 2 * TOKENS * FEATS * OUTS
+
+
+def sg_bank(g, n):
+    return False
+
+
+def t4_on_vector(g):
+    return False
 
 
 def tile_attentionalpoolerwmasking_pa_t_kernel(tc, x, ln_k_w, ln_k_b, Wk, Wv, bk, bv, out_0, out_1):
@@ -32,22 +43,164 @@ def tile_attentionalpoolerwmasking_pa_t_kernel(tc, x, ln_k_w, ln_k_b, Wk, Wv, bk
     vf = out_1.flatten_outer_dims()
 
     with ExitStack() as ctx:
+        ctx.enter_context(tc.manual_schedule())
         const = ctx.enter_context(tc.tile_pool(name="const", bufs=1))
         xin = ctx.enter_context(tc.tile_pool(name="xin", bufs=NG))
         small = ctx.enter_context(tc.tile_pool(name="small", bufs=6))
-        xh = ctx.enter_context(tc.tile_pool(name="xh", bufs=3))
-        pl = ctx.enter_context(tc.tile_pool(name="pl", bufs=3))
+        xh = ctx.enter_context(tc.tile_pool(name="xh", bufs=2))
+        pl = ctx.enter_context(tc.tile_pool(name="pl", bufs=2))
         gr = ctx.enter_context(tc.tile_pool(name="gr", bufs=3))
-        cd = ctx.enter_context(tc.tile_pool(name="cd", bufs=3))
-        rs = ctx.enter_context(tc.tile_pool(name="rs", bufs=4))
+        cd = ctx.enter_context(tc.tile_pool(name="cd", bufs=2))
+        rs = ctx.enter_context(tc.tile_pool(name="rs", bufs=3))
         psum = ctx.enter_context(tc.psum_pool(name="psum", bufs=4))
 
-        x_tiles = []
-        for g in range(NG):
-            x_sb = xin.tile([P, NT, FEATS], BF16, tag="x", name="x_sb%d" % g)
-            x_tiles.append(x_sb)
-        nc.sync.dma_start(out=x_tiles[0][:], in_=xf[0:GROUP, :].rearrange("(p n) f -> p n f", n=NT))
+        st = {}
 
+        def load(g):
+            x_sb = xin.tile([P, NT, FEATS], BF16, tag="x", name="x_sb%d" % g)
+            st[("x", g)] = x_sb
+            nc.sync.dma_start(
+                out=x_sb[:], in_=xf[g * GROUP : (g + 1) * GROUP, :].rearrange("(p n) f -> p n f", n=NT)
+            )
+
+        def stats_open(g):
+            st[("bn", g)] = small.tile([P, NT, 6], FP32, tag="bn", name="bn%d" % g)
+
+        def stats_tile(g, n):
+            nc.vector.bn_stats(out=st[("bn", g)][:, n, :], in_=st[("x", g)][:, n, :])
+
+        def stats_close(g):
+            mv = small.tile([P, NT, 2], FP32, tag="mv", name="mv%d" % g)
+            for n in range(NT):
+                nc.vector.bn_aggr(out=mv[:, n, :], in_=st[("bn", g)][:, n, :])
+            st[("mv", g)] = mv
+
+        def neg_mean(g):
+            negm = small.tile([P, NT], FP32, tag="negm", name="negm%d" % g)
+            nc.gpsimd.tensor_scalar(
+                out=negm[:], in0=st[("mv", g)][:, :, 0], scalar1=-1.0, scalar2=0.0, op0=ALU.mult, op1=ALU.add
+            )
+            st[("negm", g)] = negm
+
+        def root(g):
+            std = small.tile([P, NT], FP32, tag="std", name="std%d" % g)
+            nc.scalar.activation(out=std[:], in_=st[("mv", g)][:, :, 1], func=ACT.Sqrt, bias=EPS, scale=1.0)
+            st[("std", g)] = std
+
+        def recip(g):
+            rstd = small.tile([P, NT], FP32, tag="rstd", name="rstd%d" % g)
+            nc.vector.reciprocal(out=rstd[:], in_=st[("std", g)][:])
+            st[("rstd", g)] = rstd
+
+        def normalise(g):
+            xhat = xh.tile([P, NT, FEATS], FP32, tag="xhat", name="xhat%d" % g)
+            for n in range(NT):
+                nc.gpsimd.tensor_scalar(
+                    out=xhat[:, n, :],
+                    in0=st[("x", g)][:, n, :],
+                    scalar1=st[("negm", g)][:, n : n + 1],
+                    scalar2=st[("rstd", g)][:, n : n + 1],
+                    op0=ALU.add,
+                    op1=ALU.mult,
+                )
+            st[("xhat", g)] = xhat
+
+        def transposes(g):
+            xhat = st[("xhat", g)]
+            banks = []
+            for j in range(PACK):
+                tb = psum.tile([P, GROUP], FP32, tag="t", name="tb%d_%d" % (g, j))
+                banks.append(tb)
+            for j in range(PACK):
+                for n in range(NT):
+                    nc.tensor.transpose(
+                        banks[j][:, n * P : (n + 1) * P], xhat[:, n, j * P : (j + 1) * P], ident_f[:]
+                    )
+            st[("banks", g)] = banks
+
+        def affine(g):
+            planes = pl.tile([P, PACK, GROUP], BF16, tag="planes", name="planes%d" % g)
+            for j in range(PACK):
+                nc.scalar.activation(
+                    out=planes[:, j, :],
+                    in_=st[("banks", g)][j][:],
+                    func=ACT.Identity,
+                    scale=ln_col[:, j : j + 1],
+                    bias=ln_col[:, PACK + j : PACK + j + 1],
+                )
+            st[("planes", g)] = planes
+
+        def regroup(g):
+            grouped = gr.tile([P, GROUP, PACK], BF16, tag="grouped", name="grouped%d" % g, align_bytes=64)
+            dst = grouped[:].rearrange("p (c i) t -> p c t i", i=4)
+            src = st[("planes", g)][:].rearrange("p t (c i) -> p c t i", i=4)
+            if t4_on_vector(g):
+                nc.vector.tensor_copy(out=dst, in_=src)
+            else:
+                nc.scalar.copy(out=dst, in_=src)
+            st[("grouped", g)] = grouped
+
+        def quantise(g):
+            codes = cd.tile([P, GROUP], U32, tag="codes", name="codes%d" % g, align_bytes=64)
+            scl = cd.tile([P, GROUP], U8, tag="scl", name="scl%d" % g, align_bytes=64)
+            nc.vector.quantize_mx(
+                out=codes[:].bitcast(FP8X4),
+                scales=scl[:],
+                in_=st[("grouped", g)][:].rearrange("p c t -> p (c t)"),
+            )
+            st[("codes", g)] = codes
+            st[("scl", g)] = scl
+
+        def project(g):
+            obs = []
+            for n in range(NT):
+                ob = psum.tile([P, OUTS], FP32, tag="o", name="ob%d_%d" % (g, n))
+                nc.tensor.matmul_mx(
+                    out=ob[:],
+                    lhsT=st[("codes", g)][:, n * P : (n + 1) * P].bitcast(FP8X4),
+                    lhsT_scale=st[("scl", g)][:, n * P : (n + 1) * P],
+                    rhs=w_codes[:].bitcast(FP8X4),
+                    rhs_scale=w_scales[:],
+                    start=True,
+                    stop=True,
+                )
+                obs.append(ob)
+            st[("obs", g)] = obs
+
+        def finish(g):
+            res = rs.tile([P, 2, NT, HALF], FP32, tag="res", name="res%d" % g)
+            bias_v = bias_sb[:].rearrange("p (h o) -> p h o", h=2)
+            for n in range(NT):
+                ob_v = st[("obs", g)][n][:].rearrange("p (h o) -> p h o", h=2)
+                if sg_bank(g, n):
+                    nc.scalar.copy(out=res[:, :, n, :], in_=ob_v)
+                    nc.gpsimd.tensor_tensor(out=res[:, :, n, :], in0=res[:, :, n, :], in1=bias_v, op=ALU.add)
+                else:
+                    nc.vector.tensor_tensor(out=res[:, :, n, :], in0=ob_v, in1=bias_v, op=ALU.add)
+            rows = slice(g * GROUP, (g + 1) * GROUP)
+            nc.sync.dma_start(out=kf[rows, :].rearrange("(p n) o -> p n o", n=NT), in_=res[:, 0, :, :])
+            nc.sync.dma_start(out=vf[rows, :].rearrange("(p n) o -> p n o", n=NT), in_=res[:, 1, :, :])
+
+        def stats(g):
+            stats_open(g)
+            for n in range(NT):
+                stats_tile(g, n)
+            stats_close(g)
+
+        def scalars_and_normalise(g):
+            recip(g)
+            neg_mean(g)
+            normalise(g)
+
+        def live(g):
+            return 0 <= g < NG
+
+        x_first = xin.tile([P, NT, FEATS], BF16, tag="x", name="x_sb0")
+        st[("x", 0)] = x_first
+        for n in range(NT):
+            nc.sync.dma_start(
+                out=x_first[:, n, :], in_=xf[0:GROUP, :].rearrange("(p n) f -> p n f", n=NT)[:, n, :]
+            )
         w_raw = const.tile([P, 4, FEATS], BF16)
         nc.scalar.dma_start(out=w_raw[:, 0:2, :], in_=Wk.rearrange("(c p) f -> p c f", p=P))
         nc.scalar.dma_start(out=w_raw[:, 2:4, :], in_=Wv.rearrange("(c p) f -> p c f", p=P))
@@ -55,19 +208,23 @@ def tile_attentionalpoolerwmasking_pa_t_kernel(tc, x, ln_k_w, ln_k_b, Wk, Wv, bk
         nc.vector.memset(ln_rows[:], 0.0)
         nc.scalar.dma_start(out=ln_rows[0:4, :], in_=ln_k_w.rearrange("(j p) -> j p", p=P))
         nc.scalar.dma_start(out=ln_rows[4:8, :], in_=ln_k_b.rearrange("(j p) -> j p", p=P))
-        bias_sb = const.tile([P, OUTS], BF16)
-        nc.scalar.dma_start(out=bias_sb[:, 0:HALF], in_=bk.partition_broadcast(P))
-        nc.scalar.dma_start(out=bias_sb[:, HALF:OUTS], in_=bv.partition_broadcast(P))
-
         for g in range(1, NG):
-            nc.sync.dma_start(
-                out=x_tiles[g][:], in_=xf[g * GROUP : (g + 1) * GROUP, :].rearrange("(p n) f -> p n f", n=NT)
-            )
-
-        ident_f = const.tile([P, P], FP32)
-        make_identity(nc, ident_f[:])
+            load(g)
         ident_b = const.tile([P, P], BF16)
         make_identity(nc, ident_b[:])
+        ident_f = const.tile([P, P], FP32)
+        make_identity(nc, ident_f[:])
+
+        stats(0)
+        root(0)
+        stats_open(1)
+        stats_tile(1, 0)
+        scalars_and_normalise(0)
+
+        ln_t = psum.tile([P, P], BF16, tag="t")
+        nc.tensor.transpose(ln_t[:], ln_rows[:], ident_b[:])
+        ln_col = const.tile([P, 8], FP32)
+        nc.scalar.copy(out=ln_col[:], in_=ln_t[:, 0:8])
 
         w_grp = const.tile([P, OUTS, PACK], BF16, align_bytes=64)
         for h in range(2):
@@ -77,98 +234,45 @@ def tile_attentionalpoolerwmasking_pa_t_kernel(tc, x, ln_k_w, ln_k_b, Wk, Wv, bk
                     nc.tensor.transpose(
                         wt[:, j, c * P : (c + 1) * P], w_raw[:, 2 * h + c, j * P : (j + 1) * P], ident_b[:]
                     )
-            nc.vector.tensor_copy(
-                out=w_grp[:, h * HALF : (h + 1) * HALF, :], in_=wt[:].rearrange("p j o -> p o j")
-            )
+            nc.scalar.copy(out=w_grp[:, h * HALF : (h + 1) * HALF, :], in_=wt[:].rearrange("p j o -> p o j"))
         w_codes = const.tile([P, OUTS], U32, align_bytes=64)
         w_scales = const.tile([P, OUTS], U8, align_bytes=64)
-        nc.vector.quantize_mx(
-            out=w_codes[:].bitcast(FP8X4), scales=w_scales[:], in_=w_grp[:].rearrange("p o j -> p (o j)")
-        )
+        bias_sb = const.tile([P, OUTS], BF16)
 
-        ln_t = psum.tile([P, P], BF16, tag="t")
-        nc.tensor.transpose(ln_t[:], ln_rows[:], ident_b[:])
-        ln_col = const.tile([P, 8], FP32)
-        nc.vector.tensor_copy(out=ln_col[:], in_=ln_t[:, 0:8])
+        transposes(0)
+        for n in range(1, NT):
+            stats_tile(1, n)
+        stats_close(1)
+        root(1)
+        stats_open(2)
+        stats_tile(2, 0)
+        scalars_and_normalise(1)
+        nc.scalar.dma_start(out=bias_sb[:, 0:HALF], in_=bk.partition_broadcast(P))
+        nc.scalar.dma_start(out=bias_sb[:, HALF:OUTS], in_=bv.partition_broadcast(P))
+        for n in range(1, NT):
+            stats_tile(2, n)
+        stats_close(2)
 
-        for g in range(NG):
-            x_sb = x_tiles[g]
-            stats = small.tile([P, NT, 6], FP32)
-            mv = small.tile([P, NT, 2], FP32)
-            for n in range(NT):
-                nc.vector.bn_stats(out=stats[:, n, :], in_=x_sb[:, n, :])
-            for n in range(NT):
-                nc.vector.bn_aggr(out=mv[:, n, :], in_=stats[:, n, :])
-            std = small.tile([P, NT], FP32)
-            nc.scalar.activation(out=std[:], in_=mv[:, :, 1], func=ACT.Sqrt, bias=EPS, scale=1.0)
-            rstd = small.tile([P, NT], FP32)
-            nc.vector.reciprocal(out=rstd[:], in_=std[:])
-            negm = small.tile([P, NT], FP32)
-            nc.gpsimd.tensor_scalar(
-                out=negm[:], in0=mv[:, :, 0], scalar1=-1.0, scalar2=0.0, op0=ALU.mult, op1=ALU.add
-            )
-
-            xhat = xh.tile([P, NT, FEATS], FP32)
-            for n in range(NT):
-                nc.gpsimd.tensor_scalar(
-                    out=xhat[:, n, :],
-                    in0=x_sb[:, n, :],
-                    scalar1=negm[:, n : n + 1],
-                    scalar2=rstd[:, n : n + 1],
-                    op0=ALU.add,
-                    op1=ALU.mult,
+        for i in range(NG + 2):
+            if live(i):
+                affine(i)
+            if live(i + 1):
+                transposes(i + 1)
+            if live(i + 2):
+                root(i + 2)
+            if live(i):
+                regroup(i)
+            if live(i + 3):
+                stats(i + 3)
+            if live(i + 2):
+                scalars_and_normalise(i + 2)
+            if i == 0:
+                nc.vector.quantize_mx(
+                    out=w_codes[:].bitcast(FP8X4), scales=w_scales[:], in_=w_grp[:].rearrange("p o j -> p (o j)")
                 )
-
-            banks = []
-            for j in range(PACK):
-                tb = psum.tile([P, GROUP], FP32, tag="t", name="tb%d" % j)
-                banks.append(tb)
-            for n in range(NT):
-                for j in range(PACK):
-                    nc.tensor.transpose(
-                        banks[j][:, n * P : (n + 1) * P], xhat[:, n, j * P : (j + 1) * P], ident_f[:]
-                    )
-
-            planes = pl.tile([P, PACK, GROUP], BF16)
-            for j in range(PACK):
-                nc.scalar.activation(
-                    out=planes[:, j, :],
-                    in_=banks[j][:],
-                    func=ACT.Identity,
-                    scale=ln_col[:, j : j + 1],
-                    bias=ln_col[:, PACK + j : PACK + j + 1],
-                )
-
-            grouped = gr.tile([P, GROUP, PACK], BF16, align_bytes=64)
-            nc.scalar.copy(
-                out=grouped[:].rearrange("p (c i) t -> p c t i", i=4),
-                in_=planes[:].rearrange("p t (c i) -> p c t i", i=4),
-            )
-
-            codes = cd.tile([P, GROUP], U32, align_bytes=64)
-            scl = cd.tile([P, GROUP], U8, align_bytes=64)
-            nc.vector.quantize_mx(
-                out=codes[:].bitcast(FP8X4), scales=scl[:], in_=grouped[:].rearrange("p c t -> p (c t)")
-            )
-
-            res = rs.tile([P, 2, NT, HALF], FP32)
-            for n in range(NT):
-                ob = psum.tile([P, OUTS], FP32, tag="o")
-                nc.tensor.matmul_mx(
-                    out=ob[:],
-                    lhsT=codes[:, n * P : (n + 1) * P].bitcast(FP8X4),
-                    lhsT_scale=scl[:, n * P : (n + 1) * P],
-                    rhs=w_codes[:].bitcast(FP8X4),
-                    rhs_scale=w_scales[:],
-                    start=True,
-                    stop=True,
-                )
-                nc.vector.tensor_tensor(
-                    out=res[:, :, n, :],
-                    in0=ob[:].rearrange("p (h o) -> p h o", h=2),
-                    in1=bias_sb[:].rearrange("p (h o) -> p h o", h=2),
-                    op=ALU.add,
-                )
-            rows = slice(g * GROUP, (g + 1) * GROUP)
-            nc.sync.dma_start(out=kf[rows, :].rearrange("(p n) o -> p n o", n=NT), in_=res[:, 0, :, :])
-            nc.sync.dma_start(out=vf[rows, :].rearrange("(p n) o -> p n o", n=NT), in_=res[:, 1, :, :])
+            if live(i - 1):
+                quantise(i - 1)
+            if live(i - 2):
+                finish(i - 2)
+            if live(i - 1):
+                project(i - 1)

@@ -21,6 +21,7 @@ NT = 4
 GROUP = NT * P
 NG = TOKENS // GROUP
 EPS = 1e-5
+T4_SCALAR_TOKENS = 320
 LC = 2
 LE = 3
 LQ = 4
@@ -111,11 +112,12 @@ def tile_attentionalpoolerwmasking_pa_t_kernel(tc, x, ln_k_w, ln_k_b, Wk, Wv, bk
             for j in range(PACK):
                 tb = psum.tile([P, GROUP], FP32, tag="t", name="tb%d_%d" % (g, j))
                 banks.append(tb)
-            for j in range(PACK):
-                for n in range(NT):
-                    nc.tensor.transpose(
-                        banks[j][:, n * P : (n + 1) * P], xhat[:, n, j * P : (j + 1) * P], ident_f[:]
-                    )
+            if g == 0:
+                pairs = [(n, j) for n in range(NT) for j in range(PACK)]
+            else:
+                pairs = [(n, j) for j in range(PACK) for n in range(NT)]
+            for n, j in pairs:
+                nc.tensor.transpose(banks[j][:, n * P : (n + 1) * P], xhat[:, n, j * P : (j + 1) * P], ident_f[:])
             st[("banks", g)] = banks
 
         def affine(g):
@@ -132,12 +134,20 @@ def tile_attentionalpoolerwmasking_pa_t_kernel(tc, x, ln_k_w, ln_k_b, Wk, Wv, bk
 
         def regroup(g):
             grouped = gr.tile([P, GROUP, PACK], BF16, tag="grouped", name="grouped%d" % g, align_bytes=64)
-            dst = grouped[:].rearrange("p (c i) t -> p c t i", i=4)
-            src = st[("planes", g)][:].rearrange("p t (c i) -> p c t i", i=4)
-            if t4_on_vector(g):
-                nc.vector.tensor_copy(out=dst, in_=src)
-            else:
-                nc.scalar.copy(out=dst, in_=src)
+            planes = st[("planes", g)]
+            cut = T4_SCALAR_TOKENS
+            nc.scalar.copy(
+                out=grouped[:, 0:cut, :].rearrange("p (c i) t -> p c t i", i=4),
+                in_=planes[:, :, 0:cut].rearrange("p t (c i) -> p c t i", i=4),
+            )
+            nc.gpsimd.tensor_scalar(
+                out=grouped[:, cut:GROUP, :].rearrange("p (c i) t -> p c t i", i=4),
+                in0=planes[:, :, cut:GROUP].rearrange("p t (c i) -> p c t i", i=4),
+                scalar1=1.0,
+                scalar2=0.0,
+                op0=ALU.mult,
+                op1=ALU.add,
+            )
             st[("grouped", g)] = grouped
 
         def quantise(g):
@@ -177,9 +187,18 @@ def tile_attentionalpoolerwmasking_pa_t_kernel(tc, x, ln_k_w, ln_k_b, Wk, Wv, bk
                     nc.gpsimd.tensor_tensor(out=res[:, :, n, :], in0=res[:, :, n, :], in1=bias_v, op=ALU.add)
                 else:
                     nc.vector.tensor_tensor(out=res[:, :, n, :], in0=ob_v, in1=bias_v, op=ALU.add)
-            rows = slice(g * GROUP, (g + 1) * GROUP)
-            nc.sync.dma_start(out=kf[rows, :].rearrange("(p n) o -> p n o", n=NT), in_=res[:, 0, :, :])
-            nc.sync.dma_start(out=vf[rows, :].rearrange("(p n) o -> p n o", n=NT), in_=res[:, 1, :, :])
+                if g == NG - 1:
+                    rows = slice(g * GROUP, (g + 1) * GROUP)
+                    nc.sync.dma_start(
+                        out=kf[rows, :].rearrange("(p n) o -> p n o", n=NT)[:, n, :], in_=res[:, 0, n, :]
+                    )
+                    nc.sync.dma_start(
+                        out=vf[rows, :].rearrange("(p n) o -> p n o", n=NT)[:, n, :], in_=res[:, 1, n, :]
+                    )
+            if g < NG - 1:
+                rows = slice(g * GROUP, (g + 1) * GROUP)
+                nc.sync.dma_start(out=kf[rows, :].rearrange("(p n) o -> p n o", n=NT), in_=res[:, 0, :, :])
+                nc.sync.dma_start(out=vf[rows, :].rearrange("(p n) o -> p n o", n=NT), in_=res[:, 1, :, :])
 
         def stats(g):
             stats_open(g)
@@ -254,12 +273,12 @@ def tile_attentionalpoolerwmasking_pa_t_kernel(tc, x, ln_k_w, ln_k_b, Wk, Wv, bk
         stats_close(2)
 
         for i in range(NG + 2):
+            if live(i + 2):
+                root(i + 2)
             if live(i):
                 affine(i)
             if live(i + 1):
                 transposes(i + 1)
-            if live(i + 2):
-                root(i + 2)
             if live(i):
                 regroup(i)
             if live(i + 3):

@@ -21,7 +21,6 @@ NT = 4
 GROUP = NT * P
 NG = TOKENS // GROUP
 EPS = 1e-5
-T4_SCALAR_TOKENS = 320
 LC = 2
 LE = 3
 LQ = 4
@@ -30,7 +29,7 @@ FLOPS = 2 * TOKENS * FEATS * OUTS
 
 
 def sg_bank(g, n):
-    return False
+    return n == 3 and g % 2 == 0
 
 
 def t4_on_vector(g):
@@ -52,7 +51,7 @@ def tile_attentionalpoolerwmasking_pa_t_kernel(tc, x, ln_k_w, ln_k_b, Wk, Wv, bk
         pl = ctx.enter_context(tc.tile_pool(name="pl", bufs=2))
         gr = ctx.enter_context(tc.tile_pool(name="gr", bufs=3))
         cd = ctx.enter_context(tc.tile_pool(name="cd", bufs=2))
-        rs = ctx.enter_context(tc.tile_pool(name="rs", bufs=3))
+        rs = ctx.enter_context(tc.tile_pool(name="rs", bufs=4))
         psum = ctx.enter_context(tc.psum_pool(name="psum", bufs=4))
 
         st = {}
@@ -112,12 +111,11 @@ def tile_attentionalpoolerwmasking_pa_t_kernel(tc, x, ln_k_w, ln_k_b, Wk, Wv, bk
             for j in range(PACK):
                 tb = psum.tile([P, GROUP], FP32, tag="t", name="tb%d_%d" % (g, j))
                 banks.append(tb)
-            if g == 0:
-                pairs = [(n, j) for n in range(NT) for j in range(PACK)]
-            else:
-                pairs = [(n, j) for j in range(PACK) for n in range(NT)]
-            for n, j in pairs:
-                nc.tensor.transpose(banks[j][:, n * P : (n + 1) * P], xhat[:, n, j * P : (j + 1) * P], ident_f[:])
+            for j in range(PACK):
+                for n in range(NT):
+                    nc.tensor.transpose(
+                        banks[j][:, n * P : (n + 1) * P], xhat[:, n, j * P : (j + 1) * P], ident_f[:]
+                    )
             st[("banks", g)] = banks
 
         def affine(g):
@@ -134,20 +132,12 @@ def tile_attentionalpoolerwmasking_pa_t_kernel(tc, x, ln_k_w, ln_k_b, Wk, Wv, bk
 
         def regroup(g):
             grouped = gr.tile([P, GROUP, PACK], BF16, tag="grouped", name="grouped%d" % g, align_bytes=64)
-            planes = st[("planes", g)]
-            cut = T4_SCALAR_TOKENS
-            nc.scalar.copy(
-                out=grouped[:, 0:cut, :].rearrange("p (c i) t -> p c t i", i=4),
-                in_=planes[:, :, 0:cut].rearrange("p t (c i) -> p c t i", i=4),
-            )
-            nc.gpsimd.tensor_scalar(
-                out=grouped[:, cut:GROUP, :].rearrange("p (c i) t -> p c t i", i=4),
-                in0=planes[:, :, cut:GROUP].rearrange("p t (c i) -> p c t i", i=4),
-                scalar1=1.0,
-                scalar2=0.0,
-                op0=ALU.mult,
-                op1=ALU.add,
-            )
+            dst = grouped[:].rearrange("p (c i) t -> p c t i", i=4)
+            src = st[("planes", g)][:].rearrange("p t (c i) -> p c t i", i=4)
+            if t4_on_vector(g):
+                nc.vector.tensor_copy(out=dst, in_=src)
+            else:
+                nc.scalar.copy(out=dst, in_=src)
             st[("grouped", g)] = grouped
 
         def quantise(g):
@@ -187,18 +177,9 @@ def tile_attentionalpoolerwmasking_pa_t_kernel(tc, x, ln_k_w, ln_k_b, Wk, Wv, bk
                     nc.gpsimd.tensor_tensor(out=res[:, :, n, :], in0=res[:, :, n, :], in1=bias_v, op=ALU.add)
                 else:
                     nc.vector.tensor_tensor(out=res[:, :, n, :], in0=ob_v, in1=bias_v, op=ALU.add)
-                if g == NG - 1:
-                    rows = slice(g * GROUP, (g + 1) * GROUP)
-                    nc.sync.dma_start(
-                        out=kf[rows, :].rearrange("(p n) o -> p n o", n=NT)[:, n, :], in_=res[:, 0, n, :]
-                    )
-                    nc.sync.dma_start(
-                        out=vf[rows, :].rearrange("(p n) o -> p n o", n=NT)[:, n, :], in_=res[:, 1, n, :]
-                    )
-            if g < NG - 1:
-                rows = slice(g * GROUP, (g + 1) * GROUP)
-                nc.sync.dma_start(out=kf[rows, :].rearrange("(p n) o -> p n o", n=NT), in_=res[:, 0, :, :])
-                nc.sync.dma_start(out=vf[rows, :].rearrange("(p n) o -> p n o", n=NT), in_=res[:, 1, :, :])
+            rows = slice(g * GROUP, (g + 1) * GROUP)
+            nc.sync.dma_start(out=kf[rows, :].rearrange("(p n) o -> p n o", n=NT), in_=res[:, 0, :, :])
+            nc.sync.dma_start(out=vf[rows, :].rearrange("(p n) o -> p n o", n=NT), in_=res[:, 1, :, :])
 
         def stats(g):
             stats_open(g)
@@ -273,12 +254,12 @@ def tile_attentionalpoolerwmasking_pa_t_kernel(tc, x, ln_k_w, ln_k_b, Wk, Wv, bk
         stats_close(2)
 
         for i in range(NG + 2):
-            if live(i + 2):
-                root(i + 2)
             if live(i):
                 affine(i)
             if live(i + 1):
                 transposes(i + 1)
+            if live(i + 2):
+                root(i + 2)
             if live(i):
                 regroup(i)
             if live(i + 3):

@@ -111,11 +111,12 @@ def tile_attentionalpoolerwmasking_pa_t_kernel(tc, x, ln_k_w, ln_k_b, Wk, Wv, bk
             for j in range(PACK):
                 tb = psum.tile([P, GROUP], FP32, tag="t", name="tb%d_%d" % (g, j))
                 banks.append(tb)
-            for j in range(PACK):
-                for n in range(NT):
-                    nc.tensor.transpose(
-                        banks[j][:, n * P : (n + 1) * P], xhat[:, n, j * P : (j + 1) * P], ident_f[:]
-                    )
+            if g == 0:
+                pairs = [(n, j) for n in range(NT) for j in range(PACK)]
+            else:
+                pairs = [(n, j) for j in range(PACK) for n in range(NT)]
+            for n, j in pairs:
+                nc.tensor.transpose(banks[j][:, n * P : (n + 1) * P], xhat[:, n, j * P : (j + 1) * P], ident_f[:])
             st[("banks", g)] = banks
 
         def affine(g):
@@ -132,12 +133,10 @@ def tile_attentionalpoolerwmasking_pa_t_kernel(tc, x, ln_k_w, ln_k_b, Wk, Wv, bk
 
         def regroup(g):
             grouped = gr.tile([P, GROUP, PACK], BF16, tag="grouped", name="grouped%d" % g, align_bytes=64)
-            dst = grouped[:].rearrange("p (c i) t -> p c t i", i=4)
-            src = st[("planes", g)][:].rearrange("p t (c i) -> p c t i", i=4)
-            if t4_on_vector(g):
-                nc.vector.tensor_copy(out=dst, in_=src)
-            else:
-                nc.scalar.copy(out=dst, in_=src)
+            nc.scalar.copy(
+                out=grouped[:].rearrange("p (c i) t -> p c t i", i=4),
+                in_=st[("planes", g)][:].rearrange("p t (c i) -> p c t i", i=4),
+            )
             st[("grouped", g)] = grouped
 
         def quantise(g):
@@ -177,9 +176,18 @@ def tile_attentionalpoolerwmasking_pa_t_kernel(tc, x, ln_k_w, ln_k_b, Wk, Wv, bk
                     nc.gpsimd.tensor_tensor(out=res[:, :, n, :], in0=res[:, :, n, :], in1=bias_v, op=ALU.add)
                 else:
                     nc.vector.tensor_tensor(out=res[:, :, n, :], in0=ob_v, in1=bias_v, op=ALU.add)
-            rows = slice(g * GROUP, (g + 1) * GROUP)
-            nc.sync.dma_start(out=kf[rows, :].rearrange("(p n) o -> p n o", n=NT), in_=res[:, 0, :, :])
-            nc.sync.dma_start(out=vf[rows, :].rearrange("(p n) o -> p n o", n=NT), in_=res[:, 1, :, :])
+                if g == NG - 1:
+                    rows = slice(g * GROUP, (g + 1) * GROUP)
+                    nc.sync.dma_start(
+                        out=kf[rows, :].rearrange("(p n) o -> p n o", n=NT)[:, n, :], in_=res[:, 0, n, :]
+                    )
+                    nc.sync.dma_start(
+                        out=vf[rows, :].rearrange("(p n) o -> p n o", n=NT)[:, n, :], in_=res[:, 1, n, :]
+                    )
+            if g < NG - 1:
+                rows = slice(g * GROUP, (g + 1) * GROUP)
+                nc.sync.dma_start(out=kf[rows, :].rearrange("(p n) o -> p n o", n=NT), in_=res[:, 0, :, :])
+                nc.sync.dma_start(out=vf[rows, :].rearrange("(p n) o -> p n o", n=NT), in_=res[:, 1, :, :])
 
         def stats(g):
             stats_open(g)
@@ -254,12 +262,12 @@ def tile_attentionalpoolerwmasking_pa_t_kernel(tc, x, ln_k_w, ln_k_b, Wk, Wv, bk
         stats_close(2)
 
         for i in range(NG + 2):
+            if live(i + 2):
+                root(i + 2)
             if live(i):
                 affine(i)
             if live(i + 1):
                 transposes(i + 1)
-            if live(i + 2):
-                root(i + 2)
             if live(i):
                 regroup(i)
             if live(i + 3):

from contextlib import ExitStack

import concourse.mybir as mybir
from concourse.masks import make_identity

FP32 = mybir.dt.float32
BF16 = mybir.dt.bfloat16
U32 = mybir.dt.uint32
U8 = mybir.dt.uint8
FP8X4 = mybir.dt.float8_e4m3fn_x4
ALU = mybir.AluOpType
ACT = mybir.ActivationFunctionType

P = 128
PACK = 4
FEATS = 512
TOKENS = 8192
HALF = 256
OUTS = 2 * HALF
NT = 4
GROUP = NT * P
NG = TOKENS // GROUP
EPS = 1e-5
LC = 2
LE = 3
LQ = 4

FLOPS = 2 * TOKENS * FEATS * OUTS


def sg_bank(g, n):
    return n == 3 and g % 2 == 0


def t4_on_vector(g):
    return False


def tile_attentionalpoolerwmasking_pa_t_kernel(tc, x, ln_k_w, ln_k_b, Wk, Wv, bk, bv, out_0, out_1):
    nc = tc.nc
    xf = x.flatten_outer_dims()
    kf = out_0.flatten_outer_dims()
    vf = out_1.flatten_outer_dims()

    with ExitStack() as ctx:
        ctx.enter_context(tc.manual_schedule())
        const = ctx.enter_context(tc.tile_pool(name="const", bufs=1))
        xin = ctx.enter_context(tc.tile_pool(name="xin", bufs=NG))
        small = ctx.enter_context(tc.tile_pool(name="small", bufs=6))
        xh = ctx.enter_context(tc.tile_pool(name="xh", bufs=2))
        pl = ctx.enter_context(tc.tile_pool(name="pl", bufs=2))
        gr = ctx.enter_context(tc.tile_pool(name="gr", bufs=3))
        cd = ctx.enter_context(tc.tile_pool(name="cd", bufs=2))
        rs = ctx.enter_context(tc.tile_pool(name="rs", bufs=4))
        psum = ctx.enter_context(tc.psum_pool(name="psum", bufs=4))

        st = {}

        def load(g):
            x_sb = xin.tile([P, NT, FEATS], BF16, tag="x", name="x_sb%d" % g)
            st[("x", g)] = x_sb
            nc.sync.dma_start(
                out=x_sb[:], in_=xf[g * GROUP : (g + 1) * GROUP, :].rearrange("(p n) f -> p n f", n=NT)
            )

        def stats_open(g):
            st[("bn", g)] = small.tile([P, NT, 6], FP32, tag="bn", name="bn%d" % g)

        def stats_tile(g, n):
            nc.vector.bn_stats(out=st[("bn", g)][:, n, :], in_=st[("x", g)][:, n, :])

        def stats_close(g):
            mv = small.tile([P, NT, 2], FP32, tag="mv", name="mv%d" % g)
            for n in range(NT):
                nc.vector.bn_aggr(out=mv[:, n, :], in_=st[("bn", g)][:, n, :])
            st[("mv", g)] = mv

        def neg_mean(g):
            negm = small.tile([P, NT], FP32, tag="negm", name="negm%d" % g)
            nc.gpsimd.tensor_scalar(
                out=negm[:], in0=st[("mv", g)][:, :, 0], scalar1=-1.0, scalar2=0.0, op0=ALU.mult, op1=ALU.add
            )
            st[("negm", g)] = negm

        def root(g):
            std = small.tile([P, NT], FP32, tag="std", name="std%d" % g)
            nc.scalar.activation(out=std[:], in_=st[("mv", g)][:, :, 1], func=ACT.Sqrt, bias=EPS, scale=1.0)
            st[("std", g)] = std

        def recip(g):
            rstd = small.tile([P, NT], FP32, tag="rstd", name="rstd%d" % g)
            nc.vector.reciprocal(out=rstd[:], in_=st[("std", g)][:])
            st[("rstd", g)] = rstd

        def normalise(g):
            xhat = xh.tile([P, NT, FEATS], FP32, tag="xhat", name="xhat%d" % g)
            for n in range(NT):
                nc.gpsimd.tensor_scalar(
                    out=xhat[:, n, :],
                    in0=st[("x", g)][:, n, :],
                    scalar1=st[("negm", g)][:, n : n + 1],
                    scalar2=st[("rstd", g)][:, n : n + 1],
                    op0=ALU.add,
                    op1=ALU.mult,
                )
            st[("xhat", g)] = xhat

        def transposes(g):
            xhat = st[("xhat", g)]
            banks = []
            for j in range(PACK):
                tb = psum.tile([P, GROUP], FP32, tag="t", name="tb%d_%d" % (g, j))
                banks.append(tb)
            if g == 0:
                pairs = [(n, j) for n in range(NT) for j in range(PACK)]
            else:
                pairs = [(n, j) for j in range(PACK) for n in range(NT)]
            for n, j in pairs:
                nc.tensor.transpose(banks[j][:, n * P : (n + 1) * P], xhat[:, n, j * P : (j + 1) * P], ident_f[:])
            st[("banks", g)] = banks

        def affine(g):
            planes = pl.tile([P, PACK, GROUP], BF16, tag="planes", name="planes%d" % g)
            for j in range(PACK):
                nc.scalar.activation(
                    out=planes[:, j, :],
                    in_=st[("banks", g)][j][:],
                    func=ACT.Identity,
                    scale=ln_col[:, j : j + 1],
                    bias=ln_col[:, PACK + j : PACK + j + 1],
                )
            st[("planes", g)] = planes

        def regroup(g):
            grouped = gr.tile([P, GROUP, PACK], BF16, tag="grouped", name="grouped%d" % g, align_bytes=64)
            nc.scalar.copy(
                out=grouped[:].rearrange("p (c i) t -> p c t i", i=4),
                in_=st[("planes", g)][:].rearrange("p t (c i) -> p c t i", i=4),
            )
            st[("grouped", g)] = grouped

        def quantise(g):
            codes = cd.tile([P, GROUP], U32, tag="codes", name="codes%d" % g, align_bytes=64)
            scl = cd.tile([P, GROUP], U8, tag="scl", name="scl%d" % g, align_bytes=64)
            nc.vector.quantize_mx(
                out=codes[:].bitcast(FP8X4),
                scales=scl[:],
                in_=st[("grouped", g)][:].rearrange("p c t -> p (c t)"),
            )
            st[("codes", g)] = codes
            st[("scl", g)] = scl

        def project(g):
            obs = []
            for n in range(NT):
                ob = psum.tile([P, OUTS], FP32, tag="o", name="ob%d_%d" % (g, n))
                nc.tensor.matmul_mx(
                    out=ob[:],
                    lhsT=st[("codes", g)][:, n * P : (n + 1) * P].bitcast(FP8X4),
                    lhsT_scale=st[("scl", g)][:, n * P : (n + 1) * P],
                    rhs=w_codes[:].bitcast(FP8X4),
                    rhs_scale=w_scales[:],
                    start=True,
                    stop=True,
                )
                obs.append(ob)
            st[("obs", g)] = obs

        def finish(g):
            res = rs.tile([P, 2, NT, HALF], FP32, tag="res", name="res%d" % g)
            bias_v = bias_sb[:].rearrange("p (h o) -> p h o", h=2)
            for n in range(NT):
                ob_v = st[("obs", g)][n][:].rearrange("p (h o) -> p h o", h=2)
                if sg_bank(g, n):
                    nc.scalar.copy(out=res[:, :, n, :], in_=ob_v)
                    nc.gpsimd.tensor_tensor(out=res[:, :, n, :], in0=res[:, :, n, :], in1=bias_v, op=ALU.add)
                else:
                    nc.vector.tensor_tensor(out=res[:, :, n, :], in0=ob_v, in1=bias_v, op=ALU.add)
                if g == NG - 1:
                    rows = slice(g * GROUP, (g + 1) * GROUP)
                    nc.sync.dma_start(
                        out=kf[rows, :].rearrange("(p n) o -> p n o", n=NT)[:, n, :], in_=res[:, 0, n, :]
                    )
                    nc.sync.dma_start(
                        out=vf[rows, :].rearrange("(p n) o -> p n o", n=NT)[:, n, :], in_=res[:, 1, n, :]
                    )
            if g < NG - 1:
                rows = slice(g * GROUP, (g + 1) * GROUP)
                nc.sync.dma_start(out=kf[rows, :].rearrange("(p n) o -> p n o", n=NT), in_=res[:, 0, :, :])
                nc.sync.dma_start(out=vf[rows, :].rearrange("(p n) o -> p n o", n=NT), in_=res[:, 1, :, :])

        def stats(g):
            stats_open(g)
            for n in range(NT):
                stats_tile(g, n)
            stats_close(g)

        def scalars_and_normalise(g):
            recip(g)
            neg_mean(g)
            normalise(g)

        def live(g):
            return 0 <= g < NG

        x_first = xin.tile([P, NT, FEATS], BF16, tag="x", name="x_sb0")
        st[("x", 0)] = x_first
        for n in range(NT):
            nc.sync.dma_start(
                out=x_first[:, n, :], in_=xf[0:GROUP, :].rearrange("(p n) f -> p n f", n=NT)[:, n, :]
            )
        w_raw = const.tile([P, 4, FEATS], BF16)
        nc.scalar.dma_start(out=w_raw[:, 0:2, :], in_=Wk.rearrange("(c p) f -> p c f", p=P))
        nc.scalar.dma_start(out=w_raw[:, 2:4, :], in_=Wv.rearrange("(c p) f -> p c f", p=P))
        ln_rows = const.tile([P, P], BF16)
        nc.vector.memset(ln_rows[:], 0.0)
        nc.scalar.dma_start(out=ln_rows[0:4, :], in_=ln_k_w.rearrange("(j p) -> j p", p=P))
        nc.scalar.dma_start(out=ln_rows[4:8, :], in_=ln_k_b.rearrange("(j p) -> j p", p=P))
        for g in range(1, NG):
            load(g)
        ident_b = const.tile([P, P], BF16)
        make_identity(nc, ident_b[:])
        ident_f = const.tile([P, P], FP32)
        make_identity(nc, ident_f[:])

        stats(0)
        root(0)
        stats_open(1)
        stats_tile(1, 0)
        scalars_and_normalise(0)

        ln_t = psum.tile([P, P], BF16, tag="t")
        nc.tensor.transpose(ln_t[:], ln_rows[:], ident_b[:])
        ln_col = const.tile([P, 8], FP32)
        nc.scalar.copy(out=ln_col[:], in_=ln_t[:, 0:8])

        w_grp = const.tile([P, OUTS, PACK], BF16, align_bytes=64)
        for h in range(2):
            wt = psum.tile([P, PACK, HALF], BF16, tag="t", name="wt%d" % h)
            for j in range(PACK):
                for c in range(2):
                    nc.tensor.transpose(
                        wt[:, j, c * P : (c + 1) * P], w_raw[:, 2 * h + c, j * P : (j + 1) * P], ident_b[:]
                    )
            nc.scalar.copy(out=w_grp[:, h * HALF : (h + 1) * HALF, :], in_=wt[:].rearrange("p j o -> p o j"))
        w_codes = const.tile([P, OUTS], U32, align_bytes=64)
        w_scales = const.tile([P, OUTS], U8, align_bytes=64)
        bias_sb = const.tile([P, OUTS], BF16)

        transposes(0)
        for n in range(1, NT):
            stats_tile(1, n)
        stats_close(1)
        root(1)
        stats_open(2)
        stats_tile(2, 0)
        scalars_and_normalise(1)
        nc.scalar.dma_start(out=bias_sb[:, 0:HALF], in_=bk.partition_broadcast(P))
        nc.scalar.dma_start(out=bias_sb[:, HALF:OUTS], in_=bv.partition_broadcast(P))
        for n in range(1, NT):
            stats_tile(2, n)
        stats_close(2)

        for i in range(NG + 2):
            if live(i + 2):
                root(i + 2)
            if live(i):
                affine(i)
            if live(i + 1):
                transposes(i + 1)
            if live(i):
                regroup(i)
            if live(i + 3):
                stats(i + 3)
            if live(i + 2):
                scalars_and_normalise(i + 2)
            if i == 0:
                nc.vector.quantize_mx(
                    out=w_codes[:].bitcast(FP8X4), scales=w_scales[:], in_=w_grp[:].rearrange("p o j -> p (o j)")
                )
            if live(i - 1):
                quantise(i - 1)
            if live(i - 2):
                finish(i - 2)
            if live(i - 1):
                project(i - 1)
